import numpy as np
import ml_dtypes


def mxq(x, axis, fmt="e4m3"):
    dtype, down = {"e4m3": (ml_dtypes.float8_e4m3fn, 7), "e5m2": (ml_dtypes.float8_e5m2, 14)}[fmt]
    v = np.moveaxis(np.asarray(x, np.float32).astype(ml_dtypes.bfloat16).astype(np.float64), axis, -1)
    blocks = v.reshape(v.shape[:-1] + (-1, 32))
    amax = np.abs(blocks).max(-1, keepdims=True)
    byte = np.maximum(np.where(amax > 0, np.frexp(amax)[1] - 1 + 127, 0) - down, 1)
    scale = np.exp2(byte - 127.0)
    codes = (blocks / scale).astype(np.float32).astype(dtype).astype(np.float64)
    return np.moveaxis((codes * scale).reshape(v.shape), -1, axis)


WIDE = False


def mx_kscale(k):
    if not WIDE:
        return np.ones(k)
    levels = np.array([18, -18])
    if k % 512:
        return np.exp2(np.random.permutation(np.resize(levels, k // 32))).repeat(32)
    a = np.empty((k // 512, 16))
    for p in range(k // 512):
        a[p, :8] = np.random.permutation(np.resize(levels, 8))
        for g in range(8):
            far = levels[np.abs(levels - a[p, g]) >= 10]
            a[p, g + 8] = far[np.random.randint(len(far))]
    return np.exp2(a.ravel()).repeat(32)


BF16 = ml_dtypes.bfloat16


def bf(x):
    return np.asarray(x, np.float32).astype(BF16)


def f64(x):
    return np.asarray(x).astype(np.float64)


B, C, H, W = 2, 1024, 16, 32
C2 = 2 * C
N = H * W
T = B * N


def sigmoid(v):
    return 1.0 / (1.0 + np.exp(-v))


def to_tokens(a):
    k = a.shape[1]
    return a.reshape(B, k, N).transpose(1, 0, 2).reshape(k, T)


def from_tokens(a):
    k = a.shape[0]
    return a.reshape(k, B, N).transpose(1, 0, 2).reshape(B, k, H, W)


def setup_inputs():
    s = mx_kscale(T).reshape(B, 1, H, W)
    u = mx_kscale(C)
    v = mx_kscale(C)
    hsi0 = bf(np.random.standard_normal((B, C, H, W)))
    msi0 = bf(np.random.standard_normal((B, C, H, W)))
    att1 = bf(np.random.standard_normal((B, C, H, W)) * 0.5)
    att2 = bf(np.random.standard_normal((B, C, H, W)) * 0.5)
    wg0 = bf(np.random.standard_normal((C, C2)) / np.sqrt(C2))
    bg = bf(np.random.standard_normal(C) * 0.2)
    wp0 = bf(np.random.standard_normal((C, C)) * 2.0 / np.sqrt(C))
    bp = bf(np.random.standard_normal(C) * 0.1)
    g = bf(np.random.standard_normal((B, C, H, W)) * np.exp2(np.random.randint(-6, 1, (B, 1, H, W))) * 4.0
           / s * u[None, :, None, None])
    x0 = np.concatenate([f64(hsi0), f64(msi0)], axis=1).reshape(B, C2, N)
    gate = sigmoid(f64(wg0) @ x0 + f64(bg)[None, :, None]).reshape(B, C, H, W)
    return {"hsi": bf(f64(hsi0) * s),
            "msi": bf(f64(msi0) * s),
            "att1": att1,
            "att2": att2,
            "wg": bf(f64(wg0) / v[:, None]),
            "bg": bg,
            "wp": bf(f64(wp0) * v[None, :] / u[:, None]),
            "bp": bp,
            "gate": np.asarray(gate, np.float32),
            "grad_out": g}


def reference(hsi, msi, att1, att2, wg, bg, wp, bp, gate, grad_out):
    go = to_tokens(f64(grad_out))
    gt = to_tokens(f64(gate))
    dfused = mxq(f64(wp), 0, "e4m3").T @ mxq(go, 0, "e5m2")
    dz = dfused * (to_tokens(f64(att1)) - to_tokens(f64(att2))) * gt * (1.0 - gt)
    dhsi = mxq(f64(wg)[:, :C], 0, "e4m3").T @ mxq(dz, 0, "e5m2")
    x = to_tokens(np.concatenate([f64(hsi), f64(msi)], axis=1))
    dwg = mxq(dz, 1, "e5m2") @ mxq(x, 1, "e4m3").T
    return from_tokens(dhsi), dwg

from contextlib import ExitStack

import concourse.mybir as mybir
from concourse.masks import make_identity

F32 = mybir.dt.float32
BF16 = mybir.dt.bfloat16
U32 = mybir.dt.uint32
U8 = mybir.dt.uint8
E4M3 = mybir.dt.float8_e4m3fn_x4
E5M2 = mybir.dt.float8_e5m2_x4
ADD = mybir.AluOpType.add
MULT = mybir.AluOpType.mult
SUB = mybir.AluOpType.subtract
NRAW4 = 19
NGRP = 5
NOUT = 5
NPS = {"df": 2, "d": 2, "tr": 2, "o": 2}

FLOPS = 4 * 2 * 1024 * 1024 * 1024
BYTES = 30 * 1024 * 1024

ORDER = """
Lwp 0 0
Lwp 1 0
I wp 0 0 S
I wp 1 0 V
Lgo 0 0
I go 0 0 V
Q wp 0 0
Q wp 1 0
Lgo 0 1
Lgate 0 0
Q go 0 0
La1 0 0
I go 0 1 S
H 0 0 1
La2 0 0
Lwp 1 1
H 0 0 0
Q go 0 1
D 0 0 0
W 0 0 0
D 0 0 1
I wp 1 1 S
D 0 0 2
DF 0 0 0
DF 0 0 1
W 0 0 1
Lwp 0 1
W 0 0 2
I wp 0 1 S
Lgate 1 0
Lgo 1 0
Z 0 0 0
La2 1 0
D 0 0 3
DF 0 0 2
La1 1 0
Z 0 0 1
W 0 0 3
Z 0 0 2
DF 0 0 3
Z 0 0 3
TZ 0 0 1 S
Q wp 1 1
I go 1 0 S
Q wp 0 1
Lx 3 1
Lgo 1 1
Lx 3 0
H 1 0 0
H 1 0 1
TZ 0 0 0 S
DF 1 0 0
DF 1 0 1
D 1 0 0
W 1 0 0
D 1 0 1
Lx 2 1
W 1 0 1
XT 3 1 1 S
D 1 0 2
Z 1 0 0
Z 1 0 1
D 1 0 3
Lx 2 0
Lgate 1 1
W 1 0 2
La2 1 1
Q go 1 0
W 1 0 3
DF 1 0 3
I go 1 1 S
XT 3 0 0 S
Q dzt 0 0
Q go 1 1
XT 3 1 0 S
DF 1 0 2
XT 2 1 0 S
XT 2 0 0 S
Q x 3 1
La1 1 1
Z 1 0 3
XT 2 1 1 S
XT 3 0 1 S
Z 1 0 2
XT 2 0 1 S
H 1 1 0
TZ 1 0 1 S
Q x 2 1
DF 1 1 0
Lx 1 0
Lx 1 1
DF 1 1 1
Q x 3 0
DV 1 1 0
D 1 1 3
I dz 0 0 S
H 1 1 1
Lx 0 1
D 1 1 2
XT 1 0 1 S
XT 1 0 0 S
TZ 1 0 0 S
Q x 2 0
DV 1 1 1
Lx 0 0
XT 1 1 1 S
XT 0 1 0 S
W 1 1 0
W 1 1 3
Z 1 1 0
XT 0 1 1 S
XT 1 1 0 S
W 1 1 1
Q dzt 1 0
DF 1 1 2
Lwg 0 0
Z 1 1 1
W 1 1 2
TZ 1 1 0 S
Q dz 0 0
XT 0 0 1 S
DF 1 1 3
Z 1 1 2
La2 0 1
Z 1 1 3
Lgate 0 1
DF 0 1 0
Q x 1 1
La1 0 1
TZ 1 1 1 S
Q x 1 0
Q dzt 1 1
XT 0 0 0 S
DF 0 1 1
Q x 0 0
O1 1 0 1 S d
Q x 0 1
H 0 1 0
O1 1 0 3 S o
O1 1 1 1 S tr
DV 0 1 1
Lwg 1 0
Lwg 1 1
Lwg 0 1
O1 1 0 0 S d
O1 1 1 3 S tr
O1 1 0 2 S d
O1 1 1 0 S tr
O1 1 1 2 S d
O1 1 2 0 S tr
I wg 1 0 S
D 0 1 3
DV 0 1 0
W 0 1 1
O1 1 2 1 S d
W 0 1 0
O1 1 2 2 S o
O1 1 2 3 S tr
DV 0 1 2
Z 0 1 0
H 0 1 1
Z 0 1 1
DF 0 1 3
W 0 1 2
W 0 1 3
DF 0 1 2
Z 0 1 2
Z 0 1 3
O1 1 3 1 S o
O1 1 3 0 V d
TZ 0 1 1 V
TZ 0 1 0 S
Q dzt 0 1
I dz 1 1 V
O1 1 3 2 S df
O1 1 3 3 S df
I dz 0 1 V
O1 0 0 0 S d
O1 0 0 1 S d
Q wg 1 0
O1 0 0 3 S o
O1 0 0 2 S tr
O1 0 1 0 S d
I wg 0 0 V
I wg 0 1 V
O1 0 1 1 S tr
O1 0 1 3 S tr
Q wg 0 0
O1 0 1 2 S df
O1 0 2 0 S o
I dz 1 0 V
O1 0 2 1 S tr
O1 0 2 2 S o
O1 0 2 3 S o
O1 0 3 1 S df
O1 0 3 0 S o
O1 0 3 2 S o
Q dz 1 0
Q dz 0 1
Q dz 1 1
O1 0 3 3 S d
I wg 1 1 V
O0 0 0 S d
O0 0 1 S df
O0 0 3 V tr
O0 0 2 S tr
O0 1 0 S df
O0 1 1 S tr
Q wg 1 1
O0 1 3 S tr
Q wg 0 1
O0 1 2 S o
O0 1 4 S tr
O0 1 5 V df
O0 0 4 V tr
O0 0 5 V df
O0 1 7 V tr
O0 1 6 V d
O0 0 7 V df
O0 0 6 S tr
"""


def tile_crossattentionfusion_pa_v_kernel(
    tc, hsi, msi, att1, att2, wg, bg, wp, bp, gate, grad_out, out_0, out_1
):
    nc = tc.nc

    go_v = grad_out.rearrange("b (g p j) h w -> b g p j (h w)", g=2, j=4)
    gate_v = gate.rearrange("b (g p j) h w -> b g p j (h w)", g=2, j=4)
    a1_v = att1.rearrange("b (g p j) h w -> b g p j (h w)", g=2, j=4)
    a2_v = att2.rearrange("b (g p j) h w -> b g p j (h w)", g=2, j=4)
    x_v = [t.rearrange("b (k p q) h w -> b k p q (h w)", k=2, q=4) for t in (hsi, msi)]
    wp_v = wp.rearrange("(g p j) c -> g p j c", g=2, j=4)
    wg_v = wg.rearrange("(g p j) i -> g p j i", g=2, j=4)
    out0_v = out_0.rearrange("b (i m) h w -> b m i (h w)", m=128)
    out1_v = out_1.rearrange("(g m j) i -> g j m i", g=2, j=4)

    with ExitStack() as ctx:
        const = ctx.enter_context(tc.tile_pool(name="const", bufs=1))
        raw = ctx.enter_context(tc.tile_pool(name="raw", bufs=1))
        keep = ctx.enter_context(tc.tile_pool(name="keep", bufs=1))
        stage = ctx.enter_context(tc.tile_pool(name="stage", bufs=1))
        psum = ctx.enter_context(tc.psum_pool(name="psum", bufs=2))

        ident = const.tile([128, 128], BF16, name="ident")
        nident = const.tile([128, 128], BF16, name="nident")
        ident32 = const.tile([128, 128], F32, name="ident32")
        warm = const.tile([128, 1], F32, name="warm")


        raw_t, grp, q, ps_t, dz, o_t = {}, {}, {}, {}, {}, {}

        def load4(key, view):
            t = raw.tile([128, 4, 512], BF16, name="raw4", tag="raw4", bufs=NRAW4, align_bytes=64)
            nc.sync.dma_start(out=t[:], in_=view)
            raw_t[key] = t

        def Lgo(b, g):
            load4(("go", b, g), go_v[b, g, :, :, :])

        def La1(g, b):
            load4(("a1", g, b), a1_v[b, g, :, :, :])

        def La2(g, b):
            load4(("a2", g, b), a2_v[b, g, :, :, :])

        def Lx(ch, b):
            load4(("x", ch, b), x_v[ch // 2][b, ch % 2, :, :, :])

        def Lgate(g, b):
            t = raw.tile([128, 4, 512], F32, name="gate", tag="gate", bufs=4, align_bytes=64)
            nc.sync.dma_start(out=t[:], in_=gate_v[b, g, :, :, :])
            raw_t["gate", g, b] = t

        def Lw(kind, g, h):
            t = raw.tile([128, 4, 512], BF16, name="raw4w", tag="raw4", bufs=NRAW4, align_bytes=64)
            v = wp_v if kind == "wp" else wg_v
            nc.sync.dma_start(out=t[:], in_=v[g, :, :, 512 * h : 512 * h + 512])
            raw_t[kind, g, h] = t

        def Lwp(g, h):
            Lw("wp", g, h)

        def Lwg(g, h):
            Lw("wg", g, h)

        def copy(eng, out, in_):
            if eng == "S":
                nc.scalar.copy(out=out, in_=in_)
            else:
                nc.vector.tensor_copy(out=out, in_=in_)

        def new_grp(name):
            return stage.tile([128, 2048], BF16, name=name, tag="grp", bufs=NGRP, align_bytes=64)

        def I(kind, a, b, eng):
            t = new_grp("g_" + kind)
            src = dz[a, b] if kind == "dz" else raw_t[kind, a, b]
            if kind == "wp":
                copy(
                    eng,
                    t[:].rearrange("p (i m t) -> p m t i", i=4, t=4),
                    src[:].rearrange("p t (m i) -> p m t i", i=4),
                )
            else:
                copy(
                    eng,
                    t[:].rearrange("p (c i t) -> p c t i", i=4, t=4),
                    src[:].rearrange("p t (c i) -> p c t i", i=4),
                )
            grp[kind, a, b] = t

        def Q(kind, a, b):
            fmt = E5M2 if kind in ("go", "dz", "dzt") else E4M3
            codes = keep.tile([128, 512], U32, name="c_%s%d%d" % (kind, a, b), align_bytes=64)
            scales = keep.tile([128, 512], U8, name="s_%s%d%d" % (kind, a, b), align_bytes=64)
            nc.vector.quantize_mx(out=codes[:].bitcast(fmt), scales=scales[:], in_=grp[kind, a, b][:])
            q[kind, a, b] = codes, scales

        def mm(ps, lhs, rhs, lf, rf, cols, start, stop):
            nc.tensor.matmul_mx(
                out=ps[:],
                lhsT=lhs[0][:, cols].bitcast(lf),
                lhsT_scale=lhs[1][:, cols],
                rhs=rhs[0][:].bitcast(rf),
                rhs_scale=rhs[1][:],
                start=start,
                stop=stop,
            )

        def ptile(tag):
            return psum.tile([128, 512], F32, name="ps_" + tag, tag=tag, bufs=NPS[tag])

        def DF(g, b, j):
            ps = ptile("df")
            for o in range(2):
                mm(ps, q["wp", o, g], q["go", b, o], E4M3, E5M2, slice(128 * j, 128 * j + 128), o == 0, o == 1)
            ps_t["df", g, b, j] = ps

        def D(g, b, j):
            ps = ptile("d")
            nc.tensor.matmul(ps[:], lhsT=ident[:], rhs=raw_t["a2", g, b][:, j, :], start=True, stop=False)
            nc.tensor.matmul(ps[:], lhsT=nident[:], rhs=raw_t["a1", g, b][:, j, :], start=False, stop=True)
            ps_t["d", g, b, j] = ps[:]

        def DV(g, b, j):
            t = stage.tile([128, 512], F32, name="dv", tag="dv", bufs=2, align_bytes=64)
            nc.vector.tensor_tensor(out=t[:], in0=raw_t["a2", g, b][:, j, :], in1=raw_t["a1", g, b][:, j, :], op=SUB)
            ps_t["d", g, b, j] = t[:]

        def H(g, b, h):
            t = raw_t["gate", g, b][:, 2 * h : 2 * h + 2, :]
            nc.vector.scalar_tensor_tensor(out=t, in0=t, scalar=-1.0, in1=t, op0=ADD, op1=MULT)

        def W(g, b, j):
            t = raw_t["gate", g, b][:, j, :]
            nc.vector.tensor_tensor(out=t, in0=t, in1=ps_t["d", g, b, j], op=MULT)

        def Z(g, b, j):
            if (g, b) not in dz:
                dz[g, b] = stage.tile([128, 4, 512], BF16, name="dz", tag="dz", bufs=3, align_bytes=64)
            nc.vector.tensor_tensor(
                out=dz[g, b][:, j, :].rearrange("p (u w e) -> p u w e", u=2, e=2),
                in0=raw_t["gate", g, b][:, j, :].rearrange("p (w u e) -> p u w e", u=2, e=2),
                in1=ps_t["df", g, b, j][:].rearrange("p (w u e) -> p u w e", u=2, e=2),
                op=MULT,
            )

        def turn(kind, a, b, half, words, starts, step, eng):
            if (kind, a, b) not in grp:
                grp[kind, a, b] = new_grp("g_" + kind)
            ps = ptile("tr")
            for k, s in enumerate(starts):
                nc.tensor.transpose(ps[:, 128 * k : 128 * k + 128], words[:, s : s + 127 * step + 1 : step], ident32[:])
            copy(
                eng,
                grp[kind, a, b][:, 1024 * half : 1024 * half + 1024].bitcast(F32).rearrange("p (q r u) -> p q r u", q=2, u=2),
                ps[:].rearrange("p (q u r) -> p q r u", q=2, u=2),
            )

        def TZ(g, b, half, eng):
            words = dz[g, b][:].rearrange("p j n -> p (j n)").bitcast(F32)
            starts = [256 * j + 128 * u for j in (2 * half, 2 * half + 1) for u in range(2)]
            turn("dzt", g, b, half, words, starts, 1, eng)

        def XT(ch, b, half, eng):
            words = raw_t["x", ch, b][:].rearrange("p q n -> p (q n)").bitcast(F32)
            starts = [256 * k + u for k in (2 * half, 2 * half + 1) for u in range(2)]
            turn("x", ch, b, half, words, starts, 2, eng)

        def out_tile(key):
            if key not in o_t:
                o_t[key] = [stage.tile([128, 1024], F32, name="ot", tag="ot", bufs=NOUT, align_bytes=64), 0]
            o_t[key][1] += 1
            return o_t[key]

        def O1(g, j, ch, eng, tag):
            ps = ptile(tag)
            for b in range(2):
                mm(ps, q["dzt", g, b], q["x", ch, b], E5M2, E4M3, slice(128 * j, 128 * j + 128), b == 0, b == 1)
            t, n = out_tile(("o1", g, j, ch // 2))
            k = ch % 2
            copy(
                eng,
                t[:, 512 * k : 512 * k + 512].rearrange("p (r q) -> p r q", q=4),
                ps[:].rearrange("p (q r) -> p r q", q=4),
            )
            if n == 2:
                c0 = 1024 * (ch // 2)
                nc.sync.dma_start(out=out1_v[g, j, :, c0 : c0 + 1024], in_=t[:])

        def O0(b, i, eng, tag):
            ps = ptile(tag)
            for g in range(2):
                mm(ps, q["wg", g, i // 4], q["dz", g, b], E4M3, E5M2, slice(128 * (i % 4), 128 * (i % 4) + 128), g == 0, g == 1)
            t, n = out_tile(("o0", b, i // 2))
            k = i % 2
            copy(
                eng,
                t[:, 512 * k : 512 * k + 512].rearrange("p (w u e) -> p w u e", u=2, e=2),
                ps[:].rearrange("p (u w e) -> p w u e", u=2, e=2),
            )
            if n == 2:
                i0 = 2 * (i // 2)
                nc.sync.dma_start(out=out0_v[b, :, i0 : i0 + 2, :], in_=t[:].rearrange("p (i n) -> p i n", i=2))

        run = dict(
            Lgo=Lgo, La1=La1, La2=La2, Lx=Lx, Lgate=Lgate, Lwp=Lwp, Lwg=Lwg, I=I, Q=Q,
            DF=DF, D=D, DV=DV, H=H, W=W, Z=Z, TZ=TZ, XT=XT, O1=O1, O0=O0,
        )
        with tc.manual_schedule():
            make_identity(nc, ident32[:])
            make_identity(nc, ident[:])
            nc.scalar.copy(out=warm[:], in_=ident32[:, 0:1])
            nc.vector.tensor_scalar_mul(nident[:], ident[:], -1.0)
            for line in ORDER.split("\n"):
                word = line.split(" ")
                if word[0] in run:
                    run[word[0]](*[int(w) if w in "0123456789" else w for w in word[1:]])
